import numpy as np
import ml_dtypes


def mxq(x, axis, fmt="e4m3"):
    dtype, down = {"e4m3": (ml_dtypes.float8_e4m3fn, 7), "e5m2": (ml_dtypes.float8_e5m2, 14)}[fmt]
    v = np.moveaxis(np.asarray(x, np.float32).astype(ml_dtypes.bfloat16).astype(np.float64), axis, -1)
    blocks = v.reshape(v.shape[:-1] + (-1, 32))
    amax = np.abs(blocks).max(-1, keepdims=True)
    byte = np.maximum(np.where(amax > 0, np.frexp(amax)[1] - 1 + 127, 0) - down, 1)
    scale = np.exp2(byte - 127.0)
    codes = (blocks / scale).astype(np.float32).astype(dtype).astype(np.float64)
    return np.moveaxis((codes * scale).reshape(v.shape), -1, axis)


WIDE = False


def mx_kscale(k):
    if not WIDE:
        return np.ones(k)
    levels = np.array([20, -20, 10, -10, 0])
    a = np.random.permutation(np.resize(levels, k // 512 * 4)).reshape(k // 512, 4)
    idx = np.arange(k)
    return np.exp2(a[idx // 512, idx % 128 // 32])


BF16 = ml_dtypes.bfloat16


def bf(x):
    return np.asarray(x, np.float32).astype(BF16)


def f64(x):
    return np.asarray(x).astype(np.float64)


N, N_CH, X, H = 512, 5, 512, 512
K = N_CH * H


def sigmoid(v):
    return 1.0 / (1.0 + np.exp(-v))


def gate_preact(x, x_mask, neighbour_h, W_f_in, b_f_in, W_aggr_f, b_aggr_f):
    fi = (f64(x) @ f64(W_f_in) + f64(b_f_in)) * f64(x_mask)[:, None]
    fi = np.tile(fi, (1, N_CH))
    return f64(neighbour_h).reshape(N, K) @ f64(W_aggr_f) + f64(b_aggr_f) + fi + fi


def setup_inputs():
    u = mx_kscale(K)
    x = bf(np.random.standard_normal((N, X)))
    x_mask = bf(np.random.random(N) < 0.75)
    neighbour_h = bf(np.random.standard_normal((N, N_CH, H)))
    c0 = bf(np.random.standard_normal((N, N_CH, H)))
    W_f_in = bf(np.random.standard_normal((X, H)) * 0.5 / np.sqrt(X))
    b_f_in = bf(np.random.standard_normal(H) * 0.3)
    W0 = bf(np.random.standard_normal((K, K)) / np.sqrt(K))
    b_aggr_f = bf(np.random.standard_normal(K) * 0.3)
    g = bf(np.random.standard_normal((N, H)) * np.exp2(np.random.randint(-12, 1, (N, 1))) * 16.0)
    z = gate_preact(x, x_mask, neighbour_h, W_f_in, b_f_in, W0, b_aggr_f)
    return {
        "x": x,
        "x_mask": x_mask,
        "neighbour_h": neighbour_h,
        "neighbour_c": bf(f64(c0) * u.reshape(N_CH, H)),
        "W_f_in": W_f_in,
        "b_f_in": b_f_in,
        "W_aggr_f": bf(f64(W0) / u[None, :]),
        "b_aggr_f": b_aggr_f,
        "z": np.asarray(z, np.float32),
        "grad_out": g,
    }


def reference(x, x_mask, neighbour_h, neighbour_c, W_f_in, b_f_in, W_aggr_f, b_aggr_f, z, grad_out):
    f = sigmoid(f64(z))
    dz = np.tile(f64(grad_out), (1, N_CH)) * f64(neighbour_c).reshape(N, K) * (f * (1.0 - f))
    dh = mxq(dz, 1, "e5m2") @ mxq(f64(W_aggr_f), 1, "e4m3").T
    return dh.reshape(N, N_CH, H)

@@ -1,0 +1,179 @@
+from contextlib import ExitStack
+
+from concourse import mybir
+from concourse.masks import make_identity
+
+F32 = mybir.dt.float32
+BF16 = mybir.dt.bfloat16
+U32 = mybir.dt.uint32
+U8 = mybir.dt.uint8
+E4M3_X4 = mybir.dt.float8_e4m3fn_x4
+E5M2_X4 = mybir.dt.float8_e5m2_x4
+ACT = mybir.ActivationFunctionType
+ALU = mybir.AluOpType
+
+P = 128
+NODES = 512
+CHILDREN = 5
+HIDDEN = 512
+GATES = CHILDREN * HIDDEN
+K_PASS = 512
+PASSES = GATES // K_PASS
+NODE_TILES = NODES // P
+OUT_COLS = 512
+OUT_TILES = GATES // OUT_COLS
+ROW_GROUPS = 2
+LOADS_PER_OUT_TILE = OUT_COLS // (ROW_GROUPS * P)
+WORDS = GATES // 2
+
+FLOPS = 2 * NODES * GATES * GATES
+BYTES = GATES * GATES * 2 + NODES * GATES * (4 + 2 + 4) + NODES * HIDDEN * 2
+
+
+def tile_treelstmcell_pa_v_kernel(
+    tc, x, x_mask, neighbour_h, neighbour_c, W_f_in, b_f_in, W_aggr_f, b_aggr_f, z, grad_out, out
+):
+    nc = tc.nc
+    c_flat = neighbour_c.rearrange("n k h -> n (k h)")
+    out_flat = out.rearrange("n k h -> n (k h)")
+
+    with ExitStack() as stack:
+        const = stack.enter_context(tc.tile_pool(name="const", bufs=1))
+        keep = stack.enter_context(tc.tile_pool(name="keep", bufs=1))
+        w_pool = stack.enter_context(tc.tile_pool(name="w_pool", bufs=5))
+        gate_pool = stack.enter_context(tc.tile_pool(name="gate_pool", bufs=2))
+        w_group_pool = stack.enter_context(tc.tile_pool(name="w_group_pool", bufs=6))
+        dz_group_pool = stack.enter_context(tc.tile_pool(name="dz_group_pool", bufs=4))
+        result_pool = stack.enter_context(tc.tile_pool(name="result_pool", bufs=4))
+        flip_psum = stack.enter_context(tc.psum_pool(name="flip_psum", bufs=5))
+        acc_psum = stack.enter_context(tc.psum_pool(name="acc_psum", bufs=3))
+
+        w_codes = keep.tile([P, OUT_TILES, PASSES, OUT_COLS], U32, align_bytes=64)
+        w_scales = keep.tile([P, OUT_TILES, PASSES, OUT_COLS], U8, align_bytes=64)
+        dz_codes = keep.tile([P, NODE_TILES, PASSES, P], U32, align_bytes=64)
+        dz_scales = keep.tile([P, NODE_TILES, PASSES, P], U8, align_bytes=64)
+
+        ident = const.tile([P, P], F32)
+        make_identity(nc, ident[:])
+
+        def load_gate_inputs(nt):
+            nodes = slice(nt * P, (nt + 1) * P)
+            z_tile = gate_pool.tile([P, GATES], F32)
+            nc.sync.dma_start(out=z_tile[:], in_=z[nodes, :])
+            c_tile = gate_pool.tile([P, GATES], BF16)
+            nc.sync.dma_start(out=c_tile[:], in_=c_flat[nodes, :])
+            return z_tile, c_tile
+
+        def load_w_rows(ot, half):
+            first = ot * OUT_COLS + half * ROW_GROUPS * P
+            w_raw = w_pool.tile([P, ROW_GROUPS * GATES], BF16)
+            nc.sync.dma_start(
+                out=w_raw[:].rearrange("p (r k) -> p r k", r=ROW_GROUPS),
+                in_=W_aggr_f[first : first + ROW_GROUPS * P, :].rearrange("(r p) k -> p r k", p=P),
+            )
+            return w_raw
+
+        first_gate_inputs = load_gate_inputs(0)
+        g_raw = const.tile([P, NODE_TILES * HIDDEN], BF16)
+        nc.sync.dma_start(
+            out=g_raw[:].rearrange("p (t h) -> p t h", t=NODE_TILES),
+            in_=grad_out.rearrange("(t p) h -> p t h", p=P),
+        )
+        g_words = g_raw[:].bitcast(F32)
+        neg_g = const.tile([P, NODE_TILES, P, 4], BF16)
+        for pair in range(NODE_TILES // 2):
+            g_flip = flip_psum.tile([P, 2, 2, P], F32, tag="flip")
+            for a in range(2):
+                for u in range(2):
+                    start = (2 * pair + a) * (HIDDEN // 2) + u * P
+                    nc.tensor.transpose(g_flip[:, a, u, :], g_words[:, start : start + P], ident[:])
+            for a in range(2):
+                nc.vector.tensor_scalar(
+                    out=neg_g[:, 2 * pair + a, :, :].rearrange("p n (u e) -> p n u e", e=2),
+                    in0=g_flip[:, a, :, :].bitcast(BF16).rearrange("p u (n e) -> p n u e", e=2),
+                    scalar1=-1.0,
+                    scalar2=None,
+                    op0=ALU.mult,
+                )
+
+        def quantise_gate_gradient(nt, z_tile, c_tile):
+            nc.scalar.activation(out=z_tile[:], in_=z_tile[:], func=ACT.Sigmoid)
+            nc.scalar.activation(out=z_tile[:], in_=z_tile[:], func=ACT.Square, bias=-0.5)
+            slope_c = gate_pool.tile([P, 2 * PASSES, 2, P], F32)
+            square_view = z_tile[:].rearrange("p (h w e) -> p h w e", w=P, e=2)
+            c_view = c_tile[:].rearrange("p (h w e) -> p h w e", w=P, e=2)
+            for e in range(2):
+                nc.vector.scalar_tensor_tensor(
+                    out=slope_c[:, :, e, :],
+                    in0=square_view[:, :, :, e],
+                    scalar=0.25,
+                    in1=c_view[:, :, :, e],
+                    op0=ALU.subtract,
+                    op1=ALU.mult,
+                )
+            for g in range(PASSES):
+                dz_flip = flip_psum.tile([P, 4, P], F32, tag="flip")
+                for u in range(2):
+                    for e in range(2):
+                        nc.tensor.transpose(dz_flip[:, 2 * u + e, :], slope_c[:, 2 * g + u, e, :], ident[:])
+                dz_grouped = dz_group_pool.tile([P, P, 4], BF16, align_bytes=64)
+                nc.vector.tensor_tensor(
+                    out=dz_grouped[:],
+                    in0=dz_flip[:].rearrange("p t n -> p n t"),
+                    in1=neg_g[:, nt, :, :],
+                    op=ALU.mult,
+                )
+                nc.vector.quantize_mx(
+                    out=dz_codes[:, nt, g, :].bitcast(E5M2_X4),
+                    scales=dz_scales[:, nt, g, :],
+                    in_=dz_grouped[:].rearrange("p n t -> p (n t)"),
+                )
+
+        def quantise_w_rows(ot, half, w_raw):
+            w_words = w_raw[:].bitcast(F32)
+            cols = slice(half * ROW_GROUPS * P, (half + 1) * ROW_GROUPS * P)
+            for g in range(PASSES):
+                w_flip = flip_psum.tile([P, ROW_GROUPS, 2, P], F32, tag="flip")
+                for r in range(ROW_GROUPS):
+                    for u in range(2):
+                        start = r * WORDS + g * (K_PASS // 2) + u * P
+                        nc.tensor.transpose(w_flip[:, r, u, :], w_words[:, start : start + P], ident[:])
+                w_grouped = w_group_pool.tile([P, ROW_GROUPS * P * 4], BF16, align_bytes=64)
+                nc.scalar.copy(
+                    out=w_grouped[:].bitcast(F32).rearrange("p (r c u) -> p r c u", r=ROW_GROUPS, u=2),
+                    in_=w_flip[:].rearrange("p r u c -> p r c u"),
+                )
+                nc.vector.quantize_mx(
+                    out=w_codes[:, ot, g, cols].bitcast(E4M3_X4),
+                    scales=w_scales[:, ot, g, cols],
+                    in_=w_grouped[:],
+                )
+
+        def product(nt, ot):
+            acc = acc_psum.tile([P, OUT_COLS], F32)
+            for g in range(PASSES):
+                nc.tensor.matmul_mx(
+                    out=acc[:],
+                    lhsT=dz_codes[:, nt, g, :].bitcast(E5M2_X4),
+                    lhsT_scale=dz_scales[:, nt, g, :],
+                    rhs=w_codes[:, ot, g, :].bitcast(E4M3_X4),
+                    rhs_scale=w_scales[:, ot, g, :],
+                    start=(g == 0),
+                    stop=(g == PASSES - 1),
+                )
+            result = result_pool.tile([P, OUT_COLS], F32)
+            nc.vector.tensor_copy(out=result[:], in_=acc[:])
+            nc.gpsimd.dma_start(
+                out=out_flat[nt * P : (nt + 1) * P, ot * OUT_COLS : (ot + 1) * OUT_COLS], in_=result[:]
+            )
+
+        for step in range(OUT_TILES):
+            if step < NODE_TILES:
+                z_tile, c_tile = first_gate_inputs if step == 0 else load_gate_inputs(step)
+                quantise_gate_gradient(step, z_tile, c_tile)
+                for ot in range(step):
+                    product(step, ot)
+            for half in range(LOADS_PER_OUT_TILE):
+                quantise_w_rows(step, half, load_w_rows(step, half))
+            for nt in range(min(step + 1, NODE_TILES)):
+                product(nt, step)

@@ -17,91 +17,98 @@ NODES = 512
 CHILDREN = 5
 HIDDEN = 512
 GATES = CHILDREN * HIDDEN
-K_PASS = 512
-PASSES = GATES // K_PASS
+K_PASS = HIDDEN
+PASSES = CHILDREN
 NODE_TILES = NODES // P
 OUT_COLS = 512
 OUT_TILES = GATES // OUT_COLS
 ROW_GROUPS = 2
-LOADS_PER_OUT_TILE = OUT_COLS // (ROW_GROUPS * P)
+W_UNITS = GATES // (ROW_GROUPS * P)
+UNITS_PER_OUT_TILE = W_UNITS // OUT_TILES
 WORDS = GATES // 2
+BLOCKS = NODE_TILES * CHILDREN
+BLOCKS_PER_ROUND = BLOCKS // W_UNITS
+ROUNDS = W_UNITS
 
 FLOPS = 2 * NODES * GATES * GATES
 BYTES = GATES * GATES * 2 + NODES * GATES * (4 + 2 + 4) + NODES * HIDDEN * 2
+
+
+def products_ready_after(rounds_done):
+    node_tiles = (rounds_done * BLOCKS_PER_ROUND) // CHILDREN
+    out_tiles = rounds_done // UNITS_PER_OUT_TILE
+    return [(nt, ot) for ot in range(out_tiles) for nt in range(node_tiles)]
 
 
 def tile_treelstmcell_pa_v_kernel(
     tc, x, x_mask, neighbour_h, neighbour_c, W_f_in, b_f_in, W_aggr_f, b_aggr_f, z, grad_out, out
 ):
     nc = tc.nc
-    c_flat = neighbour_c.rearrange("n k h -> n (k h)")
     out_flat = out.rearrange("n k h -> n (k h)")
 
     with ExitStack() as stack:
         const = stack.enter_context(tc.tile_pool(name="const", bufs=1))
         keep = stack.enter_context(tc.tile_pool(name="keep", bufs=1))
         w_pool = stack.enter_context(tc.tile_pool(name="w_pool", bufs=5))
-        gate_pool = stack.enter_context(tc.tile_pool(name="gate_pool", bufs=2))
+        gate_pool = stack.enter_context(tc.tile_pool(name="gate_pool", bufs=5))
+        slope_pool = stack.enter_context(tc.tile_pool(name="slope_pool", bufs=3))
         w_group_pool = stack.enter_context(tc.tile_pool(name="w_group_pool", bufs=6))
         dz_group_pool = stack.enter_context(tc.tile_pool(name="dz_group_pool", bufs=4))
         result_pool = stack.enter_context(tc.tile_pool(name="result_pool", bufs=4))
         flip_psum = stack.enter_context(tc.psum_pool(name="flip_psum", bufs=5))
         acc_psum = stack.enter_context(tc.psum_pool(name="acc_psum", bufs=3))
+        stack.enter_context(tc.manual_schedule())
 
         w_codes = keep.tile([P, OUT_TILES, PASSES, OUT_COLS], U32, align_bytes=64)
         w_scales = keep.tile([P, OUT_TILES, PASSES, OUT_COLS], U8, align_bytes=64)
         dz_codes = keep.tile([P, NODE_TILES, PASSES, P], U32, align_bytes=64)
         dz_scales = keep.tile([P, NODE_TILES, PASSES, P], U8, align_bytes=64)
+        neg_g = const.tile([P, NODE_TILES * P, 4], BF16)
 
         ident = const.tile([P, P], F32)
         make_identity(nc, ident[:])
 
-        def load_gate_inputs(nt):
-            nodes = slice(nt * P, (nt + 1) * P)
-            z_tile = gate_pool.tile([P, GATES], F32)
-            nc.sync.dma_start(out=z_tile[:], in_=z[nodes, :])
-            c_tile = gate_pool.tile([P, GATES], BF16)
-            nc.sync.dma_start(out=c_tile[:], in_=c_flat[nodes, :])
-            return z_tile, c_tile
+        gate_inputs = {}
+        slopes = {}
+        w_rows = {}
 
-        def load_w_rows(ot, half):
-            first = ot * OUT_COLS + half * ROW_GROUPS * P
+        def load_gate_inputs(rnd):
+            if rnd >= ROUNDS:
+                return
+            z_tile = gate_pool.tile([P, BLOCKS_PER_ROUND, HIDDEN], F32)
+            c_tile = gate_pool.tile([P, BLOCKS_PER_ROUND, HIDDEN], BF16)
+            for j in range(BLOCKS_PER_ROUND):
+                nt, g = divmod(rnd * BLOCKS_PER_ROUND + j, CHILDREN)
+                nodes = slice(nt * P, (nt + 1) * P)
+                nc.sync.dma_start(out=z_tile[:, j, :], in_=z[nodes, g * HIDDEN : (g + 1) * HIDDEN])
+                nc.sync.dma_start(out=c_tile[:, j, :], in_=neighbour_c[nodes, g, :])
+            gate_inputs[rnd] = (z_tile, c_tile)
+
+        def load_w_rows(rnd):
+            if rnd >= ROUNDS:
+                return
+            first = rnd * ROW_GROUPS * P
             w_raw = w_pool.tile([P, ROW_GROUPS * GATES], BF16)
             nc.sync.dma_start(
                 out=w_raw[:].rearrange("p (r k) -> p r k", r=ROW_GROUPS),
                 in_=W_aggr_f[first : first + ROW_GROUPS * P, :].rearrange("(r p) k -> p r k", p=P),
             )
-            return w_raw
+            w_rows[rnd] = w_raw
 
-        first_gate_inputs = load_gate_inputs(0)
-        g_raw = const.tile([P, NODE_TILES * HIDDEN], BF16)
-        nc.sync.dma_start(
-            out=g_raw[:].rearrange("p (t h) -> p t h", t=NODE_TILES),
-            in_=grad_out.rearrange("(t p) h -> p t h", p=P),
-        )
-        g_words = g_raw[:].bitcast(F32)
-        neg_g = const.tile([P, NODE_TILES, P, 4], BF16)
-        for pair in range(NODE_TILES // 2):
-            g_flip = flip_psum.tile([P, 2, 2, P], F32, tag="flip")
-            for a in range(2):
-                for u in range(2):
-                    start = (2 * pair + a) * (HIDDEN // 2) + u * P
-                    nc.tensor.transpose(g_flip[:, a, u, :], g_words[:, start : start + P], ident[:])
-            for a in range(2):
-                nc.vector.tensor_scalar(
-                    out=neg_g[:, 2 * pair + a, :, :].rearrange("p n (u e) -> p n u e", e=2),
-                    in0=g_flip[:, a, :, :].bitcast(BF16).rearrange("p u (n e) -> p n u e", e=2),
-                    scalar1=-1.0,
-                    scalar2=None,
-                    op0=ALU.mult,
-                )
-
-        def quantise_gate_gradient(nt, z_tile, c_tile):
+        def sigmoid_slope(rnd):
+            if rnd >= ROUNDS:
+                return
+            z_tile = gate_inputs[rnd][0]
             nc.scalar.activation(out=z_tile[:], in_=z_tile[:], func=ACT.Sigmoid)
             nc.scalar.activation(out=z_tile[:], in_=z_tile[:], func=ACT.Square, bias=-0.5)
-            slope_c = gate_pool.tile([P, 2 * PASSES, 2, P], F32)
-            square_view = z_tile[:].rearrange("p (h w e) -> p h w e", w=P, e=2)
-            c_view = c_tile[:].rearrange("p (h w e) -> p h w e", w=P, e=2)
+
+        def times_c(rnd):
+            if rnd >= ROUNDS:
+                return
+            z_tile, c_tile = gate_inputs[rnd]
+            slope_c = slope_pool.tile([P, 2 * BLOCKS_PER_ROUND, 2, P], F32)
+            square_view = z_tile[:].rearrange("p j (u w e) -> p (j u) w e", w=P, e=2)
+            c_view = c_tile[:].rearrange("p j (u w e) -> p (j u) w e", w=P, e=2)
             for e in range(2):
                 nc.vector.scalar_tensor_tensor(
                     out=slope_c[:, :, e, :],
@@ -111,69 +118,128 @@ def tile_treelstmcell_pa_v_kernel(
                     op0=ALU.subtract,
                     op1=ALU.mult,
                 )
-            for g in range(PASSES):
-                dz_flip = flip_psum.tile([P, 4, P], F32, tag="flip")
+            slopes[rnd] = slope_c
+
+        load_gate_inputs(0)
+        g_raw = const.tile([P, NODE_TILES * HIDDEN], BF16)
+        nc.sync.dma_start(
+            out=g_raw[:].rearrange("p (t h) -> p t h", t=NODE_TILES),
+            in_=grad_out.rearrange("(t p) h -> p t h", p=P),
+        )
+        load_gate_inputs(1)
+        load_w_rows(0)
+        load_gate_inputs(2)
+        load_w_rows(1)
+        sigmoid_slope(0)
+        sigmoid_slope(1)
+
+        g_words = g_raw[:].bitcast(F32)
+        g_flips = []
+        for pair in range(NODE_TILES // 2):
+            g_flip = flip_psum.tile([P, 2, 2 * P], F32, tag="flip")
+            for a in range(2):
                 for u in range(2):
-                    for e in range(2):
-                        nc.tensor.transpose(dz_flip[:, 2 * u + e, :], slope_c[:, 2 * g + u, e, :], ident[:])
-                dz_grouped = dz_group_pool.tile([P, P, 4], BF16, align_bytes=64)
-                nc.vector.tensor_tensor(
-                    out=dz_grouped[:],
-                    in0=dz_flip[:].rearrange("p t n -> p n t"),
-                    in1=neg_g[:, nt, :, :],
-                    op=ALU.mult,
-                )
-                nc.vector.quantize_mx(
-                    out=dz_codes[:, nt, g, :].bitcast(E5M2_X4),
-                    scales=dz_scales[:, nt, g, :],
-                    in_=dz_grouped[:].rearrange("p n t -> p (n t)"),
-                )
+                    start = (2 * pair + a) * (HIDDEN // 2) + u * P
+                    nc.tensor.transpose(g_flip[:, u, a * P : (a + 1) * P], g_words[:, start : start + P], ident[:])
+            g_flips.append(g_flip)
 
-        def quantise_w_rows(ot, half, w_raw):
-            w_words = w_raw[:].bitcast(F32)
-            cols = slice(half * ROW_GROUPS * P, (half + 1) * ROW_GROUPS * P)
-            for g in range(PASSES):
-                w_flip = flip_psum.tile([P, ROW_GROUPS, 2, P], F32, tag="flip")
-                for r in range(ROW_GROUPS):
-                    for u in range(2):
-                        start = r * WORDS + g * (K_PASS // 2) + u * P
-                        nc.tensor.transpose(w_flip[:, r, u, :], w_words[:, start : start + P], ident[:])
-                w_grouped = w_group_pool.tile([P, ROW_GROUPS * P * 4], BF16, align_bytes=64)
-                nc.scalar.copy(
-                    out=w_grouped[:].bitcast(F32).rearrange("p (r c u) -> p r c u", r=ROW_GROUPS, u=2),
-                    in_=w_flip[:].rearrange("p r u c -> p r c u"),
-                )
-                nc.vector.quantize_mx(
-                    out=w_codes[:, ot, g, cols].bitcast(E4M3_X4),
-                    scales=w_scales[:, ot, g, cols],
-                    in_=w_grouped[:],
-                )
-
-        def product(nt, ot):
-            acc = acc_psum.tile([P, OUT_COLS], F32)
-            for g in range(PASSES):
-                nc.tensor.matmul_mx(
-                    out=acc[:],
-                    lhsT=dz_codes[:, nt, g, :].bitcast(E5M2_X4),
-                    lhsT_scale=dz_scales[:, nt, g, :],
-                    rhs=w_codes[:, ot, g, :].bitcast(E4M3_X4),
-                    rhs_scale=w_scales[:, ot, g, :],
-                    start=(g == 0),
-                    stop=(g == PASSES - 1),
-                )
-            result = result_pool.tile([P, OUT_COLS], F32)
-            nc.vector.tensor_copy(out=result[:], in_=acc[:])
-            nc.gpsimd.dma_start(
-                out=out_flat[nt * P : (nt + 1) * P, ot * OUT_COLS : (ot + 1) * OUT_COLS], in_=result[:]
+        def negate_g(pair):
+            nc.vector.tensor_scalar(
+                out=neg_g[:, 2 * pair * P : 2 * (pair + 1) * P, :].rearrange("p n (u e) -> p n u e", e=2),
+                in0=g_flips[pair][:].bitcast(BF16).rearrange("p u (n e) -> p n u e", e=2),
+                scalar1=-1.0,
+                scalar2=None,
+                op0=ALU.mult,
             )
 
-        for step in range(OUT_TILES):
-            if step < NODE_TILES:
-                z_tile, c_tile = first_gate_inputs if step == 0 else load_gate_inputs(step)
-                quantise_gate_gradient(step, z_tile, c_tile)
-                for ot in range(step):
-                    product(step, ot)
-            for half in range(LOADS_PER_OUT_TILE):
-                quantise_w_rows(step, half, load_w_rows(step, half))
-            for nt in range(min(step + 1, NODE_TILES)):
-                product(nt, step)
+        negate_g(0)
+        times_c(0)
+        negate_g(1)
+
+        for rnd in range(ROUNDS + 1):
+            preparing = rnd < ROUNDS
+            load_gate_inputs(rnd + 3)
+            load_w_rows(rnd + 2)
+
+            dz_flips = []
+            w_flips = []
+            if preparing:
+                for j in range(BLOCKS_PER_ROUND):
+                    dz_flip = flip_psum.tile([P, 4, P], F32, tag="flip")
+                    for u in range(2):
+                        for e in range(2):
+                            nc.tensor.transpose(dz_flip[:, 2 * u + e, :], slopes[rnd][:, 2 * j + u, e, :], ident[:])
+                    dz_flips.append(dz_flip)
+                w_words = w_rows[rnd][:].bitcast(F32)
+                for g in range(PASSES):
+                    w_flip = flip_psum.tile([P, ROW_GROUPS, 2, P], F32, tag="flip")
+                    for r in range(ROW_GROUPS):
+                        for u in range(2):
+                            start = r * WORDS + g * (K_PASS // 2) + u * P
+                            nc.tensor.transpose(w_flip[:, r, u, :], w_words[:, start : start + P], ident[:])
+                    w_flips.append(w_flip)
+
+            earlier = products_ready_after(rnd - 1) if rnd > 0 else []
+            products = [pair for pair in products_ready_after(rnd) if pair not in earlier]
+            accs = []
+            for nt, ot in products:
+                acc = acc_psum.tile([P, OUT_COLS], F32)
+                for g in range(PASSES):
+                    nc.tensor.matmul_mx(
+                        out=acc[:],
+                        lhsT=dz_codes[:, nt, g, :].bitcast(E5M2_X4),
+                        lhsT_scale=dz_scales[:, nt, g, :],
+                        rhs=w_codes[:, ot, g, :].bitcast(E4M3_X4),
+                        rhs_scale=w_scales[:, ot, g, :],
+                        start=(g == 0),
+                        stop=(g == PASSES - 1),
+                    )
+                accs.append(acc)
+
+            if preparing:
+                dz_groups = []
+                for j in range(BLOCKS_PER_ROUND):
+                    nt = (rnd * BLOCKS_PER_ROUND + j) // CHILDREN
+                    dz_grouped = dz_group_pool.tile([P, P, 4], BF16, align_bytes=64)
+                    nc.vector.tensor_tensor(
+                        out=dz_grouped[:],
+                        in0=dz_flips[j][:].rearrange("p t n -> p n t"),
+                        in1=neg_g[:, nt * P : (nt + 1) * P, :],
+                        op=ALU.mult,
+                    )
+                    dz_groups.append(dz_grouped)
+                for j in range(BLOCKS_PER_ROUND):
+                    nt, g = divmod(rnd * BLOCKS_PER_ROUND + j, CHILDREN)
+                    nc.vector.quantize_mx(
+                        out=dz_codes[:, nt, g, :].bitcast(E5M2_X4),
+                        scales=dz_scales[:, nt, g, :],
+                        in_=dz_groups[j][:].rearrange("p n t -> p (n t)"),
+                    )
+                times_c(rnd + 1)
+
+            ot_now, half = divmod(rnd, UNITS_PER_OUT_TILE)
+            cols = slice(half * ROW_GROUPS * P, (half + 1) * ROW_GROUPS * P)
+            w_groups = []
+            for step in range(max(PASSES + 1 if preparing else 0, len(products))):
+                if preparing and step < PASSES:
+                    w_grouped = w_group_pool.tile([P, ROW_GROUPS * P * 4], BF16, align_bytes=64)
+                    nc.scalar.copy(
+                        out=w_grouped[:].bitcast(F32).rearrange("p (r c u) -> p r c u", r=ROW_GROUPS, u=2),
+                        in_=w_flips[step][:].rearrange("p r u c -> p r c u"),
+                    )
+                    w_groups.append(w_grouped)
+                if preparing and 1 <= step <= PASSES:
+                    g = step - 1
+                    nc.vector.quantize_mx(
+                        out=w_codes[:, ot_now, g, cols].bitcast(E4M3_X4),
+                        scales=w_scales[:, ot_now, g, cols],
+                        in_=w_groups[g][:],
+                    )
+                if step < len(products):
+                    nt, ot = products[step]
+                    result = result_pool.tile([P, OUT_COLS], F32)
+                    nc.vector.tensor_copy(out=result[:], in_=accs[step][:])
+                    nc.gpsimd.dma_start(
+                        out=out_flat[nt * P : (nt + 1) * P, ot * OUT_COLS : (ot + 1) * OUT_COLS], in_=result[:]
+                    )
+            sigmoid_slope(rnd + 2)

@@ -27,16 +27,21 @@ W_UNITS = GATES // (ROW_GROUPS * P)
 UNITS_PER_OUT_TILE = W_UNITS // OUT_TILES
 WORDS = GATES // 2
 BLOCKS = NODE_TILES * CHILDREN
-BLOCKS_PER_ROUND = BLOCKS // W_UNITS
+BLOCKS_PER_ROUND = 3
 ROUNDS = W_UNITS
+PRODUCTS_PER_ROUND = 2
 
 FLOPS = 2 * NODES * GATES * GATES
 BYTES = GATES * GATES * 2 + NODES * GATES * (4 + 2 + 4) + NODES * HIDDEN * 2
 
 
+def blocks_of(rnd):
+    return list(range(min(BLOCKS, rnd * BLOCKS_PER_ROUND), min(BLOCKS, (rnd + 1) * BLOCKS_PER_ROUND)))
+
+
 def products_ready_after(rounds_done):
-    node_tiles = (rounds_done * BLOCKS_PER_ROUND) // CHILDREN
-    out_tiles = rounds_done // UNITS_PER_OUT_TILE
+    node_tiles = min(BLOCKS, rounds_done * BLOCKS_PER_ROUND) // CHILDREN
+    out_tiles = min(ROUNDS, rounds_done) // UNITS_PER_OUT_TILE
     return [(nt, ot) for ot in range(out_tiles) for nt in range(node_tiles)]
 
 
@@ -73,12 +78,12 @@ def tile_treelstmcell_pa_v_kernel(
         w_rows = {}
 
         def load_gate_inputs(rnd):
-            if rnd >= ROUNDS:
+            if not blocks_of(rnd):
                 return
             z_tile = gate_pool.tile([P, BLOCKS_PER_ROUND, HIDDEN], F32)
             c_tile = gate_pool.tile([P, BLOCKS_PER_ROUND, HIDDEN], BF16)
-            for j in range(BLOCKS_PER_ROUND):
-                nt, g = divmod(rnd * BLOCKS_PER_ROUND + j, CHILDREN)
+            for j, block in enumerate(blocks_of(rnd)):
+                nt, g = divmod(block, CHILDREN)
                 nodes = slice(nt * P, (nt + 1) * P)
                 nc.sync.dma_start(out=z_tile[:, j, :], in_=z[nodes, g * HIDDEN : (g + 1) * HIDDEN])
                 nc.sync.dma_start(out=c_tile[:, j, :], in_=neighbour_c[nodes, g, :])
@@ -96,22 +101,24 @@ def tile_treelstmcell_pa_v_kernel(
             w_rows[rnd] = w_raw
 
         def sigmoid_slope(rnd):
-            if rnd >= ROUNDS:
+            count = len(blocks_of(rnd))
+            if count == 0:
                 return
-            z_tile = gate_inputs[rnd][0]
-            nc.scalar.activation(out=z_tile[:], in_=z_tile[:], func=ACT.Sigmoid)
-            nc.scalar.activation(out=z_tile[:], in_=z_tile[:], func=ACT.Square, bias=-0.5)
+            z_used = gate_inputs[rnd][0][:, :count, :]
+            nc.scalar.activation(out=z_used, in_=z_used, func=ACT.Sigmoid)
+            nc.scalar.activation(out=z_used, in_=z_used, func=ACT.Square, bias=-0.5)
 
         def times_c(rnd):
-            if rnd >= ROUNDS:
+            count = len(blocks_of(rnd))
+            if count == 0:
                 return
             z_tile, c_tile = gate_inputs[rnd]
             slope_c = slope_pool.tile([P, 2 * BLOCKS_PER_ROUND, 2, P], F32)
-            square_view = z_tile[:].rearrange("p j (u w e) -> p (j u) w e", w=P, e=2)
-            c_view = c_tile[:].rearrange("p j (u w e) -> p (j u) w e", w=P, e=2)
+            square_view = z_tile[:, :count, :].rearrange("p j (u w e) -> p (j u) w e", w=P, e=2)
+            c_view = c_tile[:, :count, :].rearrange("p j (u w e) -> p (j u) w e", w=P, e=2)
             for e in range(2):
                 nc.vector.scalar_tensor_tensor(
-                    out=slope_c[:, :, e, :],
+                    out=slope_c[:, : 2 * count, e, :],
                     in0=square_view[:, :, :, e],
                     scalar=0.25,
                     in1=c_view[:, :, :, e],
@@ -156,20 +163,45 @@ def tile_treelstmcell_pa_v_kernel(
         times_c(0)
         negate_g(1)
 
+        waiting = []
         for rnd in range(ROUNDS + 1):
             preparing = rnd < ROUNDS
+            blocks = blocks_of(rnd)
             load_gate_inputs(rnd + 3)
             load_w_rows(rnd + 2)
+            earlier = products_ready_after(rnd - 1) if rnd > 0 else []
+            waiting.extend([pair for pair in products_ready_after(rnd) if pair not in earlier])
+            count = min(len(waiting), PRODUCTS_PER_ROUND) if preparing else len(waiting)
+            products = waiting[:count]
+            waiting = waiting[count:]
+            accs = []
 
+            def multiply(pairs):
+                for nt, ot in pairs:
+                    acc = acc_psum.tile([P, OUT_COLS], F32)
+                    for g in range(PASSES):
+                        nc.tensor.matmul_mx(
+                            out=acc[:],
+                            lhsT=dz_codes[:, nt, g, :].bitcast(E5M2_X4),
+                            lhsT_scale=dz_scales[:, nt, g, :],
+                            rhs=w_codes[:, ot, g, :].bitcast(E4M3_X4),
+                            rhs_scale=w_scales[:, ot, g, :],
+                            start=(g == 0),
+                            stop=(g == PASSES - 1),
+                        )
+                    accs.append(acc)
+
+            first_half = (count + 1) // 2
             dz_flips = []
+            for j in range(len(blocks)):
+                dz_flip = flip_psum.tile([P, 4, P], F32, tag="flip")
+                for u in range(2):
+                    for e in range(2):
+                        nc.tensor.transpose(dz_flip[:, 2 * u + e, :], slopes[rnd][:, 2 * j + u, e, :], ident[:])
+                dz_flips.append(dz_flip)
+            multiply(products[:first_half])
             w_flips = []
             if preparing:
-                for j in range(BLOCKS_PER_ROUND):
-                    dz_flip = flip_psum.tile([P, 4, P], F32, tag="flip")
-                    for u in range(2):
-                        for e in range(2):
-                            nc.tensor.transpose(dz_flip[:, 2 * u + e, :], slopes[rnd][:, 2 * j + u, e, :], ident[:])
-                    dz_flips.append(dz_flip)
                 w_words = w_rows[rnd][:].bitcast(F32)
                 for g in range(PASSES):
                     w_flip = flip_psum.tile([P, ROW_GROUPS, 2, P], F32, tag="flip")
@@ -178,49 +210,32 @@ def tile_treelstmcell_pa_v_kernel(
                             start = r * WORDS + g * (K_PASS // 2) + u * P
                             nc.tensor.transpose(w_flip[:, r, u, :], w_words[:, start : start + P], ident[:])
                     w_flips.append(w_flip)
+            multiply(products[first_half:])
 
-            earlier = products_ready_after(rnd - 1) if rnd > 0 else []
-            products = [pair for pair in products_ready_after(rnd) if pair not in earlier]
-            accs = []
-            for nt, ot in products:
-                acc = acc_psum.tile([P, OUT_COLS], F32)
-                for g in range(PASSES):
-                    nc.tensor.matmul_mx(
-                        out=acc[:],
-                        lhsT=dz_codes[:, nt, g, :].bitcast(E5M2_X4),
-                        lhsT_scale=dz_scales[:, nt, g, :],
-                        rhs=w_codes[:, ot, g, :].bitcast(E4M3_X4),
-                        rhs_scale=w_scales[:, ot, g, :],
-                        start=(g == 0),
-                        stop=(g == PASSES - 1),
-                    )
-                accs.append(acc)
-
-            if preparing:
-                dz_groups = []
-                for j in range(BLOCKS_PER_ROUND):
-                    nt = (rnd * BLOCKS_PER_ROUND + j) // CHILDREN
-                    dz_grouped = dz_group_pool.tile([P, P, 4], BF16, align_bytes=64)
-                    nc.vector.tensor_tensor(
-                        out=dz_grouped[:],
-                        in0=dz_flips[j][:].rearrange("p t n -> p n t"),
-                        in1=neg_g[:, nt * P : (nt + 1) * P, :],
-                        op=ALU.mult,
-                    )
-                    dz_groups.append(dz_grouped)
-                for j in range(BLOCKS_PER_ROUND):
-                    nt, g = divmod(rnd * BLOCKS_PER_ROUND + j, CHILDREN)
-                    nc.vector.quantize_mx(
-                        out=dz_codes[:, nt, g, :].bitcast(E5M2_X4),
-                        scales=dz_scales[:, nt, g, :],
-                        in_=dz_groups[j][:].rearrange("p n t -> p (n t)"),
-                    )
-                times_c(rnd + 1)
+            dz_groups = []
+            for j, block in enumerate(blocks):
+                nt = block // CHILDREN
+                dz_grouped = dz_group_pool.tile([P, P, 4], BF16, align_bytes=64)
+                nc.vector.tensor_tensor(
+                    out=dz_grouped[:],
+                    in0=dz_flips[j][:].rearrange("p t n -> p n t"),
+                    in1=neg_g[:, nt * P : (nt + 1) * P, :],
+                    op=ALU.mult,
+                )
+                dz_groups.append(dz_grouped)
+            for j, block in enumerate(blocks):
+                nt, g = divmod(block, CHILDREN)
+                nc.vector.quantize_mx(
+                    out=dz_codes[:, nt, g, :].bitcast(E5M2_X4),
+                    scales=dz_scales[:, nt, g, :],
+                    in_=dz_groups[j][:].rearrange("p n t -> p (n t)"),
+                )
+            times_c(rnd + 1)
 
             ot_now, half = divmod(rnd, UNITS_PER_OUT_TILE)
             cols = slice(half * ROW_GROUPS * P, (half + 1) * ROW_GROUPS * P)
             w_groups = []
-            for step in range(max(PASSES + 1 if preparing else 0, len(products))):
+            for step in range(max(PASSES + 1 if preparing else 0, count)):
                 if preparing and step < PASSES:
                     w_grouped = w_group_pool.tile([P, ROW_GROUPS * P * 4], BF16, align_bytes=64)
                     nc.scalar.copy(
@@ -235,7 +250,7 @@ def tile_treelstmcell_pa_v_kernel(
                         scales=w_scales[:, ot_now, g, cols],
                         in_=w_groups[g][:],
                     )
-                if step < len(products):
+                if step < count:
                     nt, ot = products[step]
                     result = result_pool.tile([P, OUT_COLS], F32)
                     nc.vector.tensor_copy(out=result[:], in_=accs[step][:])

@@ -84,9 +84,10 @@ def tile_treelstmcell_pa_v_kernel(
             c_tile = gate_pool.tile([P, BLOCKS_PER_ROUND, HIDDEN], BF16)
             for j, block in enumerate(blocks_of(rnd)):
                 nt, g = divmod(block, CHILDREN)
-                nodes = slice(nt * P, (nt + 1) * P)
-                nc.sync.dma_start(out=z_tile[:, j, :], in_=z[nodes, g * HIDDEN : (g + 1) * HIDDEN])
-                nc.sync.dma_start(out=c_tile[:, j, :], in_=neighbour_c[nodes, g, :])
+                nc.sync.dma_start(out=z_tile[:, j, :], in_=z[nt * P : (nt + 1) * P, g * HIDDEN : (g + 1) * HIDDEN])
+            for j, block in enumerate(blocks_of(rnd)):
+                nt, g = divmod(block, CHILDREN)
+                nc.sync.dma_start(out=c_tile[:, j, :], in_=neighbour_c[nt * P : (nt + 1) * P, g, :])
             gate_inputs[rnd] = (z_tile, c_tile)
 
         def load_w_rows(rnd):
@@ -254,7 +255,7 @@ def tile_treelstmcell_pa_v_kernel(
                     nt, ot = products[step]
                     result = result_pool.tile([P, OUT_COLS], F32)
                     nc.vector.tensor_copy(out=result[:], in_=accs[step][:])
-                    nc.gpsimd.dma_start(
+                    nc.sync.dma_start(
                         out=out_flat[nt * P : (nt + 1) * P, ot * OUT_COLS : (ot + 1) * OUT_COLS], in_=result[:]
                     )
             sigmoid_slope(rnd + 2)

@@ -27,7 +27,9 @@ W_UNITS = GATES // (ROW_GROUPS * P)
 UNITS_PER_OUT_TILE = W_UNITS // OUT_TILES
 WORDS = GATES // 2
 BLOCKS = NODE_TILES * CHILDREN
-BLOCKS_PER_ROUND = 3
+MOST_BLOCKS = 3
+FEWER_BLOCKS = 2
+FULL_ROUNDS = 2
 ROUNDS = W_UNITS
 PRODUCTS_PER_ROUND = 2
 
@@ -35,12 +37,17 @@ FLOPS = 2 * NODES * GATES * GATES
 BYTES = GATES * GATES * 2 + NODES * GATES * (4 + 2 + 4) + NODES * HIDDEN * 2
 
 
+def blocks_before(rnd):
+    full = min(rnd, FULL_ROUNDS)
+    return min(BLOCKS, full * MOST_BLOCKS + (rnd - full) * FEWER_BLOCKS)
+
+
 def blocks_of(rnd):
-    return list(range(min(BLOCKS, rnd * BLOCKS_PER_ROUND), min(BLOCKS, (rnd + 1) * BLOCKS_PER_ROUND)))
+    return list(range(blocks_before(rnd), blocks_before(rnd + 1)))
 
 
 def products_ready_after(rounds_done):
-    node_tiles = min(BLOCKS, rounds_done * BLOCKS_PER_ROUND) // CHILDREN
+    node_tiles = blocks_before(rounds_done) // CHILDREN
     out_tiles = min(ROUNDS, rounds_done) // UNITS_PER_OUT_TILE
     return [(nt, ot) for ot in range(out_tiles) for nt in range(node_tiles)]
 
@@ -70,6 +77,10 @@ def tile_treelstmcell_pa_v_kernel(
         dz_scales = keep.tile([P, NODE_TILES, PASSES, P], U8, align_bytes=64)
         neg_g = const.tile([P, NODE_TILES * P, 4], BF16)
 
+        warm = const.tile([P, 1], F32)
+        nc.vector.memset(warm[:], 0.0)
+        nc.scalar.activation(out=warm[:], in_=warm[:], func=ACT.Sigmoid)
+
         ident = const.tile([P, P], F32)
         make_identity(nc, ident[:])
 
@@ -80,8 +91,8 @@ def tile_treelstmcell_pa_v_kernel(
         def load_gate_inputs(rnd):
             if not blocks_of(rnd):
                 return
-            z_tile = gate_pool.tile([P, BLOCKS_PER_ROUND, HIDDEN], F32)
-            c_tile = gate_pool.tile([P, BLOCKS_PER_ROUND, HIDDEN], BF16)
+            z_tile = gate_pool.tile([P, MOST_BLOCKS, HIDDEN], F32)
+            c_tile = gate_pool.tile([P, MOST_BLOCKS, HIDDEN], BF16)
             for j, block in enumerate(blocks_of(rnd)):
                 nt, g = divmod(block, CHILDREN)
                 nc.sync.dma_start(out=z_tile[:, j, :], in_=z[nt * P : (nt + 1) * P, g * HIDDEN : (g + 1) * HIDDEN])
@@ -114,7 +125,7 @@ def tile_treelstmcell_pa_v_kernel(
             if count == 0:
                 return
             z_tile, c_tile = gate_inputs[rnd]
-            slope_c = slope_pool.tile([P, 2 * BLOCKS_PER_ROUND, 2, P], F32)
+            slope_c = slope_pool.tile([P, 2 * MOST_BLOCKS, 2, P], F32)
             square_view = z_tile[:, :count, :].rearrange("p j (u w e) -> p (j u) w e", w=P, e=2)
             c_view = c_tile[:, :count, :].rearrange("p j (u w e) -> p (j u) w e", w=P, e=2)
             for e in range(2):

@@ -244,6 +244,17 @@ def tile_treelstmcell_pa_v_kernel(
                 )
             times_c(rnd + 1)
 
+            def empty_product(index):
+                nt, ot = products[index]
+                result = result_pool.tile([P, OUT_COLS], F32)
+                if index % 2 == 0:
+                    nc.vector.tensor_copy(out=result[:], in_=accs[index][:])
+                else:
+                    nc.scalar.copy(out=result[:], in_=accs[index][:])
+                nc.sync.dma_start(
+                    out=out_flat[nt * P : (nt + 1) * P, ot * OUT_COLS : (ot + 1) * OUT_COLS], in_=result[:]
+                )
+
             ot_now, half = divmod(rnd, UNITS_PER_OUT_TILE)
             cols = slice(half * ROW_GROUPS * P, (half + 1) * ROW_GROUPS * P)
             w_groups = []
@@ -262,11 +273,9 @@ def tile_treelstmcell_pa_v_kernel(
                         scales=w_scales[:, ot_now, g, cols],
                         in_=w_groups[g][:],
                     )
-                if step < count:
-                    nt, ot = products[step]
-                    result = result_pool.tile([P, OUT_COLS], F32)
-                    nc.vector.tensor_copy(out=result[:], in_=accs[step][:])
-                    nc.sync.dma_start(
-                        out=out_flat[nt * P : (nt + 1) * P, ot * OUT_COLS : (ot + 1) * OUT_COLS], in_=result[:]
-                    )
+                if step < count and (step % 2 == 0 or not preparing):
+                    empty_product(step)
+            if preparing:
+                for index in range(1, count, 2):
+                    empty_product(index)
             sigmoid_slope(rnd + 2)

from contextlib import ExitStack

from concourse import mybir
from concourse.masks import make_identity

F32 = mybir.dt.float32
BF16 = mybir.dt.bfloat16
U32 = mybir.dt.uint32
U8 = mybir.dt.uint8
E4M3_X4 = mybir.dt.float8_e4m3fn_x4
E5M2_X4 = mybir.dt.float8_e5m2_x4
ACT = mybir.ActivationFunctionType
ALU = mybir.AluOpType

P = 128
NODES = 512
CHILDREN = 5
HIDDEN = 512
GATES = CHILDREN * HIDDEN
K_PASS = HIDDEN
PASSES = CHILDREN
NODE_TILES = NODES // P
OUT_COLS = 512
OUT_TILES = GATES // OUT_COLS
ROW_GROUPS = 2
W_UNITS = GATES // (ROW_GROUPS * P)
UNITS_PER_OUT_TILE = W_UNITS // OUT_TILES
WORDS = GATES // 2
BLOCKS = NODE_TILES * CHILDREN
MOST_BLOCKS = 3
FEWER_BLOCKS = 2
FULL_ROUNDS = 2
ROUNDS = W_UNITS
PRODUCTS_PER_ROUND = 2

FLOPS = 2 * NODES * GATES * GATES
BYTES = GATES * GATES * 2 + NODES * GATES * (4 + 2 + 4) + NODES * HIDDEN * 2


def blocks_before(rnd):
    full = min(rnd, FULL_ROUNDS)
    return min(BLOCKS, full * MOST_BLOCKS + (rnd - full) * FEWER_BLOCKS)


def blocks_of(rnd):
    return list(range(blocks_before(rnd), blocks_before(rnd + 1)))


def products_ready_after(rounds_done):
    node_tiles = blocks_before(rounds_done) // CHILDREN
    out_tiles = min(ROUNDS, rounds_done) // UNITS_PER_OUT_TILE
    return [(nt, ot) for ot in range(out_tiles) for nt in range(node_tiles)]


def tile_treelstmcell_pa_v_kernel(
    tc, x, x_mask, neighbour_h, neighbour_c, W_f_in, b_f_in, W_aggr_f, b_aggr_f, z, grad_out, out
):
    nc = tc.nc
    out_flat = out.rearrange("n k h -> n (k h)")

    with ExitStack() as stack:
        const = stack.enter_context(tc.tile_pool(name="const", bufs=1))
        keep = stack.enter_context(tc.tile_pool(name="keep", bufs=1))
        w_pool = stack.enter_context(tc.tile_pool(name="w_pool", bufs=5))
        gate_pool = stack.enter_context(tc.tile_pool(name="gate_pool", bufs=5))
        slope_pool = stack.enter_context(tc.tile_pool(name="slope_pool", bufs=3))
        w_group_pool = stack.enter_context(tc.tile_pool(name="w_group_pool", bufs=6))
        dz_group_pool = stack.enter_context(tc.tile_pool(name="dz_group_pool", bufs=4))
        result_pool = stack.enter_context(tc.tile_pool(name="result_pool", bufs=4))
        flip_psum = stack.enter_context(tc.psum_pool(name="flip_psum", bufs=5))
        acc_psum = stack.enter_context(tc.psum_pool(name="acc_psum", bufs=3))
        stack.enter_context(tc.manual_schedule())

        w_codes = keep.tile([P, OUT_TILES, PASSES, OUT_COLS], U32, align_bytes=64)
        w_scales = keep.tile([P, OUT_TILES, PASSES, OUT_COLS], U8, align_bytes=64)
        dz_codes = keep.tile([P, NODE_TILES, PASSES, P], U32, align_bytes=64)
        dz_scales = keep.tile([P, NODE_TILES, PASSES, P], U8, align_bytes=64)
        neg_g = const.tile([P, NODE_TILES * P, 4], BF16)

        warm = const.tile([P, 1], F32)
        nc.vector.memset(warm[:], 0.0)
        nc.scalar.activation(out=warm[:], in_=warm[:], func=ACT.Sigmoid)

        ident = const.tile([P, P], F32)
        make_identity(nc, ident[:])

        gate_inputs = {}
        slopes = {}
        w_rows = {}

        def load_gate_inputs(rnd):
            if not blocks_of(rnd):
                return
            z_tile = gate_pool.tile([P, MOST_BLOCKS, HIDDEN], F32)
            c_tile = gate_pool.tile([P, MOST_BLOCKS, HIDDEN], BF16)
            for j, block in enumerate(blocks_of(rnd)):
                nt, g = divmod(block, CHILDREN)
                nc.sync.dma_start(out=z_tile[:, j, :], in_=z[nt * P : (nt + 1) * P, g * HIDDEN : (g + 1) * HIDDEN])
            for j, block in enumerate(blocks_of(rnd)):
                nt, g = divmod(block, CHILDREN)
                nc.sync.dma_start(out=c_tile[:, j, :], in_=neighbour_c[nt * P : (nt + 1) * P, g, :])
            gate_inputs[rnd] = (z_tile, c_tile)

        def load_w_rows(rnd):
            if rnd >= ROUNDS:
                return
            first = rnd * ROW_GROUPS * P
            w_raw = w_pool.tile([P, ROW_GROUPS * GATES], BF16)
            nc.sync.dma_start(
                out=w_raw[:].rearrange("p (r k) -> p r k", r=ROW_GROUPS),
                in_=W_aggr_f[first : first + ROW_GROUPS * P, :].rearrange("(r p) k -> p r k", p=P),
            )
            w_rows[rnd] = w_raw

        def sigmoid_slope(rnd):
            count = len(blocks_of(rnd))
            if count == 0:
                return
            z_used = gate_inputs[rnd][0][:, :count, :]
            nc.scalar.activation(out=z_used, in_=z_used, func=ACT.Sigmoid)
            nc.scalar.activation(out=z_used, in_=z_used, func=ACT.Square, bias=-0.5)

        def times_c(rnd):
            count = len(blocks_of(rnd))
            if count == 0:
                return
            z_tile, c_tile = gate_inputs[rnd]
            slope_c = slope_pool.tile([P, 2 * MOST_BLOCKS, 2, P], F32)
            square_view = z_tile[:, :count, :].rearrange("p j (u w e) -> p (j u) w e", w=P, e=2)
            c_view = c_tile[:, :count, :].rearrange("p j (u w e) -> p (j u) w e", w=P, e=2)
            for e in range(2):
                nc.vector.scalar_tensor_tensor(
                    out=slope_c[:, : 2 * count, e, :],
                    in0=square_view[:, :, :, e],
                    scalar=0.25,
                    in1=c_view[:, :, :, e],
                    op0=ALU.subtract,
                    op1=ALU.mult,
                )
            slopes[rnd] = slope_c

        load_gate_inputs(0)
        g_raw = const.tile([P, NODE_TILES * HIDDEN], BF16)
        nc.sync.dma_start(
            out=g_raw[:].rearrange("p (t h) -> p t h", t=NODE_TILES),
            in_=grad_out.rearrange("(t p) h -> p t h", p=P),
        )
        load_gate_inputs(1)
        load_w_rows(0)
        load_gate_inputs(2)
        load_w_rows(1)
        sigmoid_slope(0)
        sigmoid_slope(1)

        g_words = g_raw[:].bitcast(F32)
        g_flips = []
        for pair in range(NODE_TILES // 2):
            g_flip = flip_psum.tile([P, 2, 2 * P], F32, tag="flip")
            for a in range(2):
                for u in range(2):
                    start = (2 * pair + a) * (HIDDEN // 2) + u * P
                    nc.tensor.transpose(g_flip[:, u, a * P : (a + 1) * P], g_words[:, start : start + P], ident[:])
            g_flips.append(g_flip)

        def negate_g(pair):
            nc.vector.tensor_scalar(
                out=neg_g[:, 2 * pair * P : 2 * (pair + 1) * P, :].rearrange("p n (u e) -> p n u e", e=2),
                in0=g_flips[pair][:].bitcast(BF16).rearrange("p u (n e) -> p n u e", e=2),
                scalar1=-1.0,
                scalar2=None,
                op0=ALU.mult,
            )

        negate_g(0)
        times_c(0)
        negate_g(1)

        waiting = []
        for rnd in range(ROUNDS + 1):
            preparing = rnd < ROUNDS
            blocks = blocks_of(rnd)
            load_gate_inputs(rnd + 3)
            load_w_rows(rnd + 2)
            earlier = products_ready_after(rnd - 1) if rnd > 0 else []
            waiting.extend([pair for pair in products_ready_after(rnd) if pair not in earlier])
            count = min(len(waiting), PRODUCTS_PER_ROUND) if preparing else len(waiting)
            products = waiting[:count]
            waiting = waiting[count:]
            accs = []

            def multiply(pairs):
                for nt, ot in pairs:
                    acc = acc_psum.tile([P, OUT_COLS], F32)
                    for g in range(PASSES):
                        nc.tensor.matmul_mx(
                            out=acc[:],
                            lhsT=dz_codes[:, nt, g, :].bitcast(E5M2_X4),
                            lhsT_scale=dz_scales[:, nt, g, :],
                            rhs=w_codes[:, ot, g, :].bitcast(E4M3_X4),
                            rhs_scale=w_scales[:, ot, g, :],
                            start=(g == 0),
                            stop=(g == PASSES - 1),
                        )
                    accs.append(acc)

            first_half = (count + 1) // 2
            dz_flips = []
            for j in range(len(blocks)):
                dz_flip = flip_psum.tile([P, 4, P], F32, tag="flip")
                for u in range(2):
                    for e in range(2):
                        nc.tensor.transpose(dz_flip[:, 2 * u + e, :], slopes[rnd][:, 2 * j + u, e, :], ident[:])
                dz_flips.append(dz_flip)
            multiply(products[:first_half])
            w_flips = []
            if preparing:
                w_words = w_rows[rnd][:].bitcast(F32)
                for g in range(PASSES):
                    w_flip = flip_psum.tile([P, ROW_GROUPS, 2, P], F32, tag="flip")
                    for r in range(ROW_GROUPS):
                        for u in range(2):
                            start = r * WORDS + g * (K_PASS // 2) + u * P
                            nc.tensor.transpose(w_flip[:, r, u, :], w_words[:, start : start + P], ident[:])
                    w_flips.append(w_flip)
            multiply(products[first_half:])

            dz_groups = []
            for j, block in enumerate(blocks):
                nt = block // CHILDREN
                dz_grouped = dz_group_pool.tile([P, P, 4], BF16, align_bytes=64)
                nc.vector.tensor_tensor(
                    out=dz_grouped[:],
                    in0=dz_flips[j][:].rearrange("p t n -> p n t"),
                    in1=neg_g[:, nt * P : (nt + 1) * P, :],
                    op=ALU.mult,
                )
                dz_groups.append(dz_grouped)
            for j, block in enumerate(blocks):
                nt, g = divmod(block, CHILDREN)
                nc.vector.quantize_mx(
                    out=dz_codes[:, nt, g, :].bitcast(E5M2_X4),
                    scales=dz_scales[:, nt, g, :],
                    in_=dz_groups[j][:].rearrange("p n t -> p (n t)"),
                )
            times_c(rnd + 1)

            def empty_product(index):
                nt, ot = products[index]
                result = result_pool.tile([P, OUT_COLS], F32)
                if index % 2 == 0:
                    nc.vector.tensor_copy(out=result[:], in_=accs[index][:])
                else:
                    nc.scalar.copy(out=result[:], in_=accs[index][:])
                nc.sync.dma_start(
                    out=out_flat[nt * P : (nt + 1) * P, ot * OUT_COLS : (ot + 1) * OUT_COLS], in_=result[:]
                )

            ot_now, half = divmod(rnd, UNITS_PER_OUT_TILE)
            cols = slice(half * ROW_GROUPS * P, (half + 1) * ROW_GROUPS * P)
            w_groups = []
            for step in range(max(PASSES + 1 if preparing else 0, count)):
                if preparing and step < PASSES:
                    w_grouped = w_group_pool.tile([P, ROW_GROUPS * P * 4], BF16, align_bytes=64)
                    nc.scalar.copy(
                        out=w_grouped[:].bitcast(F32).rearrange("p (r c u) -> p r c u", r=ROW_GROUPS, u=2),
                        in_=w_flips[step][:].rearrange("p r u c -> p r c u"),
                    )
                    w_groups.append(w_grouped)
                if preparing and 1 <= step <= PASSES:
                    g = step - 1
                    nc.vector.quantize_mx(
                        out=w_codes[:, ot_now, g, cols].bitcast(E4M3_X4),
                        scales=w_scales[:, ot_now, g, cols],
                        in_=w_groups[g][:],
                    )
                if step < count and (step % 2 == 0 or not preparing):
                    empty_product(step)
            if preparing:
                for index in range(1, count, 2):
                    empty_product(index)
            sigmoid_slope(rnd + 2)
